import numpy as np
import ml_dtypes


def mxq(x, axis, fmt="e4m3"):
    dtype, down = {"e4m3": (ml_dtypes.float8_e4m3fn, 7), "e5m2": (ml_dtypes.float8_e5m2, 14)}[fmt]
    v = np.moveaxis(np.asarray(x, np.float32).astype(ml_dtypes.bfloat16).astype(np.float64), axis, -1)
    blocks = v.reshape(v.shape[:-1] + (-1, 32))
    amax = np.abs(blocks).max(-1, keepdims=True)
    byte = np.maximum(np.where(amax > 0, np.frexp(amax)[1] - 1 + 127, 0) - down, 1)
    scale = np.exp2(byte - 127.0)
    codes = (blocks / scale).astype(np.float32).astype(dtype).astype(np.float64)
    return np.moveaxis((codes * scale).reshape(v.shape), -1, axis)


WIDE = False


def mx_kscale(k):
    if not WIDE:
        return np.ones(k)
    levels = np.array([10, -10, 5, -5, 0])
    if k % 512:
        return np.exp2(np.random.permutation(np.resize(levels, k // 32))).repeat(32)
    a = np.empty((k // 512, 16))
    for p in range(k // 512):
        a[p, :8] = np.random.permutation(np.resize(levels, 8))
        for g in range(8):
            far = levels[np.abs(levels - a[p, g]) >= 10]
            a[p, g + 8] = far[np.random.randint(len(far))]
    return np.exp2(a.ravel()).repeat(32)


BF16 = ml_dtypes.bfloat16


def bf(x):
    return np.asarray(x, np.float32).astype(BF16)


def f64(x):
    return np.asarray(x).astype(np.float64)


G, S, M, H, E, C = 2, 512, 512, 1024, 16, 64


def setup_inputs():
    s, t = mx_kscale(S), mx_kscale(M)
    return {"dispatch_mask": bf(np.random.standard_normal((G, S, E, C)) * 0.1 * s[None, :, None, None]),
            "x": bf(np.random.standard_normal((G, S, M)) / s[None, :, None] * t),
            "wi": bf(np.random.standard_normal((E, M, H)) * 10.0 / np.sqrt(S * M) / t[None, :, None])}


def reference(dispatch_mask, x, wi):
    dm = mxq(f64(dispatch_mask).reshape(G, S, E * C), 1, "e4m3")
    xq = mxq(f64(x), 1, "e4m3")
    d = dm.transpose(0, 2, 1) @ xq
    dispatched = d.reshape(G, E, C, M).transpose(1, 0, 2, 3)
    pre = mxq(dispatched.reshape(E, G * C, M), 2, "e4m3") @ mxq(f64(wi), 1, "e4m3")
    return np.maximum(pre, 0.0).reshape(E, G, C, H)

@@ -1,0 +1,197 @@
+from contextlib import ExitStack
+
+import concourse.mybir as mybir
+
+G, S, M, H, E, C = 2, 512, 512, 1024, 16, 64
+EC = E * C
+FLOPS = 2 * G * S * EC * M + 2 * E * G * C * M * H
+
+F32 = mybir.dt.float32
+BF16 = mybir.dt.bfloat16
+U32 = mybir.dt.uint32
+U8 = mybir.dt.uint8
+FP8X4 = mybir.dt.float8_e4m3fn_x4
+RELU = mybir.ActivationFunctionType.Relu
+
+P = 128
+PACK = 4
+NB = EC // P
+HALF = 512
+BANK_DT = F32
+X_V_SLOTS = 2
+DM_V_COLS = 640
+W_V_COLS = 656
+W_V_ONLY = 1
+W_BUFS = 8
+
+
+def interleave(copy, dst, src, c0, c1):
+    copy(out=dst[:, c0:c1, :], in_=src[:, :, c0:c1].rearrange("p t c -> p c t"))
+
+
+def tile_flaxpositionwisemoelayer_pa_kernel(tc, dispatch_mask, x, wi, out):
+    nc = tc.nc
+    with ExitStack() as ctx:
+        keep = ctx.enter_context(tc.tile_pool(name="keep", bufs=1))
+        stream = ctx.enter_context(tc.tile_pool(name="stream", bufs=3))
+        psum1 = ctx.enter_context(tc.psum_pool(name="psum1", bufs=4))
+        psum2 = ctx.enter_context(tc.psum_pool(name="psum2", bufs=4))
+        ctx.enter_context(tc.manual_schedule())
+
+        x_raw, x_grouped, x_codes, x_scales = {}, {}, {}, {}
+        dm_raw, dm_grouped, dm_codes, dm_scales = {}, {}, {}, {}
+        banks, d_grouped, d_codes, d_scales = {}, {}, {}, {}
+        w_raw, w_grouped, w_codes, w_scales = {}, {}, {}, {}
+        accs, results = {}, {}
+
+        def quantize(codes, scales, grouped):
+            nc.vector.quantize_mx(out=codes.bitcast(FP8X4), scales=scales, in_=grouped)
+
+        def load_x(g):
+            x_raw[g] = keep.tile([P, PACK, M], BF16, name="x_raw%d" % g)
+            nc.sync.dma_start(out=x_raw[g][:], in_=x[g].rearrange("(p j) m -> p j m", j=PACK))
+
+        def load_dm(g):
+            dm_raw[g] = keep.tile([P, PACK, EC], BF16, name="dm_raw%d" % g)
+            nc.sync.dma_start(out=dm_raw[g][:], in_=dispatch_mask[g].rearrange("(p j) e c -> p j (e c)", j=PACK))
+
+        def load_w(e):
+            w_raw[e] = stream.tile([P, PACK, H], BF16, name="w_raw", bufs=W_BUFS)
+            nc.sync.dma_start(out=w_raw[e][:], in_=wi[e].rearrange("(p j) h -> p j h", j=PACK))
+
+        def group_x(g):
+            x_grouped[g] = keep.tile([P, PACK, P, PACK], BF16, name="x_grouped%d" % g, align_bytes=64)
+            src = x_raw[g][:].rearrange("p j (m t) -> p t m j", t=PACK)
+            nc.vector.tensor_copy(out=x_grouped[g][:, :X_V_SLOTS], in_=src[:, :X_V_SLOTS])
+            nc.scalar.copy(out=x_grouped[g][:, X_V_SLOTS:], in_=src[:, X_V_SLOTS:])
+
+        def quant_x(g):
+            x_codes[g] = keep.tile([P, M], U32, name="x_codes%d" % g, align_bytes=64)
+            x_scales[g] = keep.tile([P, M], U8, name="x_scales%d" % g, align_bytes=64)
+            quantize(x_codes[g][:], x_scales[g][:], x_grouped[g][:].rearrange("p t m j -> p (t m j)"))
+
+        def group_dm(g):
+            dm_grouped[g] = keep.tile([P, EC, PACK], BF16, name="dm_grouped%d" % g, align_bytes=64)
+            interleave(nc.vector.tensor_copy, dm_grouped[g], dm_raw[g], 0, DM_V_COLS)
+            interleave(nc.scalar.copy, dm_grouped[g], dm_raw[g], DM_V_COLS, EC)
+
+        def quant_dm(g):
+            dm_codes[g] = keep.tile([P, EC], U32, name="dm_codes%d" % g, align_bytes=64)
+            dm_scales[g] = keep.tile([P, EC], U8, name="dm_scales%d" % g, align_bytes=64)
+            quantize(dm_codes[g][:], dm_scales[g][:], dm_grouped[g][:].rearrange("p c j -> p (c j)"))
+
+        def dispatch(g, b):
+            banks[g, b] = psum1.tile([P, PACK, P], BANK_DT, name="bank")
+            for t in range(PACK):
+                nc.tensor.matmul_mx(
+                    out=banks[g, b][:, t, :],
+                    lhsT=x_codes[g][:, t * P : (t + 1) * P].bitcast(FP8X4),
+                    lhsT_scale=x_scales[g][:, t * P : (t + 1) * P],
+                    rhs=dm_codes[g][:, b * P : (b + 1) * P].bitcast(FP8X4),
+                    rhs_scale=dm_scales[g][:, b * P : (b + 1) * P],
+                    start=True,
+                    stop=True,
+                )
+
+        def empty_bank(g, b):
+            if g == 0:
+                d_grouped[b] = keep.tile([P, 2, G, C, PACK], BF16, name="d_grouped%d" % b, align_bytes=64)
+            nc.scalar.copy(
+                out=d_grouped[b][:, :, g, :, :],
+                in_=banks[g, b][:].rearrange("p t (e c) -> p e c t", e=2),
+            )
+
+        def quant_d(b):
+            d_codes[b] = keep.tile([P, 2 * P], U32, name="d_codes%d" % b, align_bytes=64)
+            d_scales[b] = keep.tile([P, 2 * P], U8, name="d_scales%d" % b, align_bytes=64)
+            quantize(d_codes[b][:], d_scales[b][:], d_grouped[b][:].rearrange("p e g c t -> p (e g c t)"))
+
+        def group_w(e):
+            w_grouped[e] = stream.tile([P, H, PACK], BF16, name="w_grouped", align_bytes=64)
+            v_cols = H if e < W_V_ONLY else W_V_COLS
+            interleave(nc.vector.tensor_copy, w_grouped[e], w_raw[e], 0, v_cols)
+            if v_cols < H:
+                interleave(nc.scalar.copy, w_grouped[e], w_raw[e], v_cols, H)
+
+        def quant_w(e):
+            w_codes[e] = stream.tile([P, H], U32, name="w_codes", align_bytes=64)
+            w_scales[e] = stream.tile([P, H], U8, name="w_scales", align_bytes=64)
+            quantize(w_codes[e][:], w_scales[e][:], w_grouped[e][:].rearrange("p c j -> p (c j)"))
+
+        def project(e):
+            b, half = e // 2, e % 2
+            for n in range(H // HALF):
+                accs[e, n] = psum2.tile([P, HALF], F32, name="acc")
+                nc.tensor.matmul_mx(
+                    out=accs[e, n][:],
+                    lhsT=d_codes[b][:, half * P : (half + 1) * P].bitcast(FP8X4),
+                    lhsT_scale=d_scales[b][:, half * P : (half + 1) * P],
+                    rhs=w_codes[e][:, n * HALF : (n + 1) * HALF].bitcast(FP8X4),
+                    rhs_scale=w_scales[e][:, n * HALF : (n + 1) * HALF],
+                    start=True,
+                    stop=True,
+                )
+
+        def relu_store(e):
+            results[e] = stream.tile([P, H], F32, name="result", bufs=4)
+            rows = out[e].rearrange("g c h -> (g c) h")
+            if e < E - 1:
+                for n in range(H // HALF):
+                    nc.scalar.activation(out=results[e][:, n * HALF : (n + 1) * HALF], in_=accs[e, n][:], func=RELU)
+                nc.sync.dma_start(out=rows, in_=results[e][:])
+            else:
+                nc.scalar.activation(out=results[e][:, :HALF], in_=accs[e, 0][:], func=RELU)
+                nc.vector.tensor_scalar_max(out=results[e][:, HALF:], in0=accs[e, 1][:], scalar1=0.0)
+                nc.sync.dma_start(out=rows[:, :HALF], in_=results[e][:, :HALF])
+                nc.sync.dma_start(out=rows[:, HALF:], in_=results[e][:, HALF:])
+
+        warm_in = keep.tile([P, 1], F32, name="warm_in")
+        warm_out = keep.tile([P, 1], F32, name="warm_out")
+        nc.gpsimd.memset(warm_in[:], 0.0)
+        nc.scalar.activation(out=warm_out[:], in_=warm_in[:], func=RELU)
+
+        load_x(0)
+        load_x(1)
+        load_dm(0)
+        load_dm(1)
+        for e in range(W_BUFS):
+            load_w(e)
+
+        group_x(0)
+        group_x(1)
+        quant_x(0)
+        group_dm(0)
+        quant_x(1)
+        quant_dm(0)
+        group_dm(1)
+        for b in range(4):
+            dispatch(0, b)
+        for b in range(4):
+            empty_bank(0, b)
+            dispatch(0, b + 4)
+        group_w(0)
+        quant_dm(1)
+        for b in range(4, NB):
+            empty_bank(0, b)
+            dispatch(1, b - 4)
+        group_w(1)
+        quant_w(0)
+        for b in range(4):
+            empty_bank(1, b)
+            dispatch(1, b + 4)
+        for b in range(4, NB):
+            empty_bank(1, b)
+        for e in range(1, E):
+            if e + 1 < E:
+                group_w(e + 1)
+            if e - 1 + W_BUFS < E:
+                load_w(e - 1 + W_BUFS)
+            if e == 1:
+                quant_d(0)
+                project(0)
+            if e % 2 == 0:
+                quant_d(e // 2)
+            quant_w(e)
+            project(e)
+            relu_store(e - 1)
+        relu_store(E - 1)

@@ -26,7 +26,10 @@ W_BUFS = 8
 
 
 def interleave(copy, dst, src, c0, c1):
-    copy(out=dst[:, c0:c1, :], in_=src[:, :, c0:c1].rearrange("p t c -> p c t"))
+    copy(
+        out=dst[:, c0:c1, :].rearrange("p (c i) t -> p c t i", i=4),
+        in_=src[:, :, c0:c1].rearrange("p t (c i) -> p c t i", i=4),
+    )
 
 
 def tile_flaxpositionwisemoelayer_pa_kernel(tc, dispatch_mask, x, wi, out):

@@ -1,6 +1,7 @@
 from contextlib import ExitStack
 
 import concourse.mybir as mybir
+from concourse.masks import make_identity
 
 G, S, M, H, E, C = 2, 512, 512, 1024, 16, 64
 EC = E * C
@@ -19,10 +20,12 @@ NB = EC // P
 HALF = 512
 BANK_DT = F32
 X_V_SLOTS = 2
-DM_V_COLS = 640
-W_V_COLS = 656
+DM_V_COLS = 352
+W_V_COLS = 608
 W_V_ONLY = 1
+LIFT_COLS = 160
 W_BUFS = 8
+BANK_BUFS = 2
 
 
 def interleave(copy, dst, src, c0, c1):
@@ -37,14 +40,23 @@ def tile_flaxpositionwisemoelayer_pa_kernel(tc, dispatch_mask, x, wi, out):
     with ExitStack() as ctx:
         keep = ctx.enter_context(tc.tile_pool(name="keep", bufs=1))
         stream = ctx.enter_context(tc.tile_pool(name="stream", bufs=3))
-        psum1 = ctx.enter_context(tc.psum_pool(name="psum1", bufs=4))
+        psum1 = ctx.enter_context(tc.psum_pool(name="psum1", bufs=BANK_BUFS))
+        psum_lift = ctx.enter_context(tc.psum_pool(name="psum_lift", bufs=2))
         psum2 = ctx.enter_context(tc.psum_pool(name="psum2", bufs=4))
+
+        ident = keep.tile([P, P], BF16, name="ident")
+        make_identity(nc, ident[:])
+        warm_in = keep.tile([P, 1], F32, name="warm_in")
+        warm_out = keep.tile([P, 1], F32, name="warm_out")
+        nc.gpsimd.memset(warm_in[:], 0.0)
+        nc.scalar.activation(out=warm_out[:], in_=warm_in[:], func=RELU)
+
         ctx.enter_context(tc.manual_schedule())
 
         x_raw, x_grouped, x_codes, x_scales = {}, {}, {}, {}
         dm_raw, dm_grouped, dm_codes, dm_scales = {}, {}, {}, {}
         banks, d_grouped, d_codes, d_scales = {}, {}, {}, {}
-        w_raw, w_grouped, w_codes, w_scales = {}, {}, {}, {}
+        w_raw, w_grouped, w_codes, w_scales, lifted = {}, {}, {}, {}, {}
         accs, results = {}, {}
 
         def quantize(codes, scales, grouped):
@@ -54,9 +66,10 @@ def tile_flaxpositionwisemoelayer_pa_kernel(tc, dispatch_mask, x, wi, out):
             x_raw[g] = keep.tile([P, PACK, M], BF16, name="x_raw%d" % g)
             nc.sync.dma_start(out=x_raw[g][:], in_=x[g].rearrange("(p j) m -> p j m", j=PACK))
 
-        def load_dm(g):
-            dm_raw[g] = keep.tile([P, PACK, EC], BF16, name="dm_raw%d" % g)
-            nc.sync.dma_start(out=dm_raw[g][:], in_=dispatch_mask[g].rearrange("(p j) e c -> p j (e c)", j=PACK))
+        def load_dm(g, h):
+            dm_raw[g, h] = keep.tile([P, PACK, HALF], BF16, name="dm_raw%d%d" % (g, h))
+            rows = dispatch_mask[g].rearrange("(p j) e c -> p j (e c)", j=PACK)
+            nc.sync.dma_start(out=dm_raw[g, h][:], in_=rows[:, :, h * HALF : (h + 1) * HALF])
 
         def load_w(e):
             w_raw[e] = stream.tile([P, PACK, H], BF16, name="w_raw", bufs=W_BUFS)
@@ -73,25 +86,27 @@ def tile_flaxpositionwisemoelayer_pa_kernel(tc, dispatch_mask, x, wi, out):
             x_scales[g] = keep.tile([P, M], U8, name="x_scales%d" % g, align_bytes=64)
             quantize(x_codes[g][:], x_scales[g][:], x_grouped[g][:].rearrange("p t m j -> p (t m j)"))
 
-        def group_dm(g):
-            dm_grouped[g] = keep.tile([P, EC, PACK], BF16, name="dm_grouped%d" % g, align_bytes=64)
-            interleave(nc.vector.tensor_copy, dm_grouped[g], dm_raw[g], 0, DM_V_COLS)
-            interleave(nc.scalar.copy, dm_grouped[g], dm_raw[g], DM_V_COLS, EC)
+        def group_dm(g, h):
+            dm_grouped[g, h] = keep.tile([P, HALF, PACK], BF16, name="dm_grouped%d%d" % (g, h), align_bytes=64)
+            interleave(nc.vector.tensor_copy, dm_grouped[g, h], dm_raw[g, h], 0, DM_V_COLS)
+            interleave(nc.scalar.copy, dm_grouped[g, h], dm_raw[g, h], DM_V_COLS, HALF)
 
-        def quant_dm(g):
-            dm_codes[g] = keep.tile([P, EC], U32, name="dm_codes%d" % g, align_bytes=64)
-            dm_scales[g] = keep.tile([P, EC], U8, name="dm_scales%d" % g, align_bytes=64)
-            quantize(dm_codes[g][:], dm_scales[g][:], dm_grouped[g][:].rearrange("p c j -> p (c j)"))
+        def quant_dm(g, h):
+            dm_codes[g, h] = keep.tile([P, HALF], U32, name="dm_codes%d%d" % (g, h), align_bytes=64)
+            dm_scales[g, h] = keep.tile([P, HALF], U8, name="dm_scales%d%d" % (g, h), align_bytes=64)
+            quantize(dm_codes[g, h][:], dm_scales[g, h][:], dm_grouped[g, h][:].rearrange("p c j -> p (c j)"))
+            ready[0] += NB // 2
 
         def dispatch(g, b):
             banks[g, b] = psum1.tile([P, PACK, P], BANK_DT, name="bank")
+            h, q = divmod(b, NB // 2)
             for t in range(PACK):
                 nc.tensor.matmul_mx(
                     out=banks[g, b][:, t, :],
                     lhsT=x_codes[g][:, t * P : (t + 1) * P].bitcast(FP8X4),
                     lhsT_scale=x_scales[g][:, t * P : (t + 1) * P],
-                    rhs=dm_codes[g][:, b * P : (b + 1) * P].bitcast(FP8X4),
-                    rhs_scale=dm_scales[g][:, b * P : (b + 1) * P],
+                    rhs=dm_codes[g, h][:, q * P : (q + 1) * P].bitcast(FP8X4),
+                    rhs_scale=dm_scales[g, h][:, q * P : (q + 1) * P],
                     start=True,
                     stop=True,
                 )
@@ -104,6 +119,20 @@ def tile_flaxpositionwisemoelayer_pa_kernel(tc, dispatch_mask, x, wi, out):
                 in_=banks[g, b][:].rearrange("p t (e c) -> p e c t", e=2),
             )
 
+        stage1 = [(g, b) for g in range(G) for b in range(NB)]
+        ready, filled, emptied = [0], [0], [0]
+
+        def fill_next():
+            if filled[0] < ready[0]:
+                dispatch(*stage1[filled[0]])
+                filled[0] += 1
+
+        def empty_next(n):
+            for i in range(n):
+                empty_bank(*stage1[emptied[0]])
+                emptied[0] += 1
+                fill_next()
+
         def quant_d(b):
             d_codes[b] = keep.tile([P, 2 * P], U32, name="d_codes%d" % b, align_bytes=64)
             d_scales[b] = keep.tile([P, 2 * P], U8, name="d_scales%d" % b, align_bytes=64)
@@ -111,10 +140,17 @@ def tile_flaxpositionwisemoelayer_pa_kernel(tc, dispatch_mask, x, wi, out):
 
         def group_w(e):
             w_grouped[e] = stream.tile([P, H, PACK], BF16, name="w_grouped", align_bytes=64)
-            v_cols = H if e < W_V_ONLY else W_V_COLS
-            interleave(nc.vector.tensor_copy, w_grouped[e], w_raw[e], 0, v_cols)
-            if v_cols < H:
-                interleave(nc.scalar.copy, w_grouped[e], w_raw[e], v_cols, H)
+            if e < W_V_ONLY:
+                interleave(nc.vector.tensor_copy, w_grouped[e], w_raw[e], 0, H)
+                return
+            lifted[e] = psum_lift.tile([P, LIFT_COLS, PACK], BF16, name="lifted")
+            src = w_raw[e][:, :, H - LIFT_COLS :].rearrange("p t c -> p c t")
+            for c0 in range(0, LIFT_COLS, P):
+                c1 = min(c0 + P, LIFT_COLS)
+                nc.tensor.matmul(out=lifted[e][:, c0:c1, :], lhsT=ident[:], rhs=src[:, c0:c1, :], start=True, stop=True)
+            interleave(nc.vector.tensor_copy, w_grouped[e], w_raw[e], 0, W_V_COLS)
+            interleave(nc.scalar.copy, w_grouped[e], w_raw[e], W_V_COLS, H - LIFT_COLS)
+            nc.scalar.copy(out=w_grouped[e][:, H - LIFT_COLS :, :], in_=lifted[e][:])
 
         def quant_w(e):
             w_codes[e] = stream.tile([P, H], U32, name="w_codes", align_bytes=64)
@@ -136,7 +172,7 @@ def tile_flaxpositionwisemoelayer_pa_kernel(tc, dispatch_mask, x, wi, out):
                 )
 
         def relu_store(e):
-            results[e] = stream.tile([P, H], F32, name="result", bufs=4)
+            results[e] = stream.tile([P, H], F32, name="result", bufs=6)
             rows = out[e].rearrange("g c h -> (g c) h")
             if e < E - 1:
                 for n in range(H // HALF):
@@ -148,42 +184,35 @@ def tile_flaxpositionwisemoelayer_pa_kernel(tc, dispatch_mask, x, wi, out):
                 nc.sync.dma_start(out=rows[:, :HALF], in_=results[e][:, :HALF])
                 nc.sync.dma_start(out=rows[:, HALF:], in_=results[e][:, HALF:])
 
-        warm_in = keep.tile([P, 1], F32, name="warm_in")
-        warm_out = keep.tile([P, 1], F32, name="warm_out")
-        nc.gpsimd.memset(warm_in[:], 0.0)
-        nc.scalar.activation(out=warm_out[:], in_=warm_in[:], func=RELU)
-
         load_x(0)
         load_x(1)
-        load_dm(0)
-        load_dm(1)
+        for g in range(G):
+            for h in range(2):
+                load_dm(g, h)
         for e in range(W_BUFS):
             load_w(e)
 
         group_x(0)
         group_x(1)
         quant_x(0)
-        group_dm(0)
+        group_dm(0, 0)
         quant_x(1)
-        quant_dm(0)
-        group_dm(1)
-        for b in range(4):
-            dispatch(0, b)
-        for b in range(4):
-            empty_bank(0, b)
-            dispatch(0, b + 4)
+        group_dm(0, 1)
+        quant_dm(0, 0)
+        for i in range(BANK_BUFS):
+            fill_next()
+        group_dm(1, 0)
+        quant_dm(0, 1)
+        empty_next(2)
+        group_dm(1, 1)
+        quant_dm(1, 0)
+        empty_next(2)
         group_w(0)
-        quant_dm(1)
-        for b in range(4, NB):
-            empty_bank(0, b)
-            dispatch(1, b - 4)
+        quant_dm(1, 1)
+        empty_next(4)
         group_w(1)
         quant_w(0)
-        for b in range(4):
-            empty_bank(1, b)
-            dispatch(1, b + 4)
-        for b in range(4, NB):
-            empty_bank(1, b)
+        empty_next(8)
         for e in range(1, E):
             if e + 1 < E:
                 group_w(e + 1)

@@ -22,10 +22,10 @@ BANK_DT = F32
 X_V_SLOTS = 2
 DM_V_COLS = 352
 W_V_COLS = 608
-W_V_ONLY = 1
-LIFT_COLS = 160
+W_V_ONLY = 2
+LIFT_COLS = 128
 W_BUFS = 8
-BANK_BUFS = 2
+BANK_BUFS = 4
 
 
 def interleave(copy, dst, src, c0, c1):
@@ -41,7 +41,6 @@ def tile_flaxpositionwisemoelayer_pa_kernel(tc, dispatch_mask, x, wi, out):
         keep = ctx.enter_context(tc.tile_pool(name="keep", bufs=1))
         stream = ctx.enter_context(tc.tile_pool(name="stream", bufs=3))
         psum1 = ctx.enter_context(tc.psum_pool(name="psum1", bufs=BANK_BUFS))
-        psum_lift = ctx.enter_context(tc.psum_pool(name="psum_lift", bufs=2))
         psum2 = ctx.enter_context(tc.psum_pool(name="psum2", bufs=4))
 
         ident = keep.tile([P, P], BF16, name="ident")
@@ -98,7 +97,7 @@ def tile_flaxpositionwisemoelayer_pa_kernel(tc, dispatch_mask, x, wi, out):
             ready[0] += NB // 2
 
         def dispatch(g, b):
-            banks[g, b] = psum1.tile([P, PACK, P], BANK_DT, name="bank")
+            banks[g, b] = psum1.tile([P, PACK, P], BANK_DT, name="bank", tag="stage")
             h, q = divmod(b, NB // 2)
             for t in range(PACK):
                 nc.tensor.matmul_mx(
@@ -138,16 +137,16 @@ def tile_flaxpositionwisemoelayer_pa_kernel(tc, dispatch_mask, x, wi, out):
             d_scales[b] = keep.tile([P, 2 * P], U8, name="d_scales%d" % b, align_bytes=64)
             quantize(d_codes[b][:], d_scales[b][:], d_grouped[b][:].rearrange("p e g c t -> p (e g c t)"))
 
+        def lift(e):
+            lifted[e] = psum1.tile([P, LIFT_COLS, PACK], BF16, name="lifted", tag="stage")
+            src = w_raw[e][:, :, H - LIFT_COLS :].rearrange("p t c -> p c t")
+            nc.tensor.matmul(out=lifted[e][:], lhsT=ident[:], rhs=src, start=True, stop=True)
+
         def group_w(e):
             w_grouped[e] = stream.tile([P, H, PACK], BF16, name="w_grouped", align_bytes=64)
             if e < W_V_ONLY:
                 interleave(nc.vector.tensor_copy, w_grouped[e], w_raw[e], 0, H)
                 return
-            lifted[e] = psum_lift.tile([P, LIFT_COLS, PACK], BF16, name="lifted")
-            src = w_raw[e][:, :, H - LIFT_COLS :].rearrange("p t c -> p c t")
-            for c0 in range(0, LIFT_COLS, P):
-                c1 = min(c0 + P, LIFT_COLS)
-                nc.tensor.matmul(out=lifted[e][:, c0:c1, :], lhsT=ident[:], rhs=src[:, c0:c1, :], start=True, stop=True)
             interleave(nc.vector.tensor_copy, w_grouped[e], w_raw[e], 0, W_V_COLS)
             interleave(nc.scalar.copy, w_grouped[e], w_raw[e], W_V_COLS, H - LIFT_COLS)
             nc.scalar.copy(out=w_grouped[e][:, H - LIFT_COLS :, :], in_=lifted[e][:])
@@ -213,7 +212,10 @@ def tile_flaxpositionwisemoelayer_pa_kernel(tc, dispatch_mask, x, wi, out):
         group_w(1)
         quant_w(0)
         empty_next(8)
+        lift(2)
         for e in range(1, E):
+            if e + 2 < E:
+                lift(e + 2)
             if e + 1 < E:
                 group_w(e + 1)
             if e - 1 + W_BUFS < E:

from contextlib import ExitStack

import concourse.mybir as mybir
from concourse.masks import make_identity

G, S, M, H, E, C = 2, 512, 512, 1024, 16, 64
EC = E * C
FLOPS = 2 * G * S * EC * M + 2 * E * G * C * M * H

F32 = mybir.dt.float32
BF16 = mybir.dt.bfloat16
U32 = mybir.dt.uint32
U8 = mybir.dt.uint8
FP8X4 = mybir.dt.float8_e4m3fn_x4
RELU = mybir.ActivationFunctionType.Relu

P = 128
PACK = 4
NB = EC // P
HALF = 512
BANK_DT = F32
X_V_SLOTS = 2
DM_V_COLS = 352
W_V_COLS = 608
W_V_ONLY = 2
LIFT_COLS = 128
W_BUFS = 8
BANK_BUFS = 4


def interleave(copy, dst, src, c0, c1):
    copy(
        out=dst[:, c0:c1, :].rearrange("p (c i) t -> p c t i", i=4),
        in_=src[:, :, c0:c1].rearrange("p t (c i) -> p c t i", i=4),
    )


def tile_flaxpositionwisemoelayer_pa_kernel(tc, dispatch_mask, x, wi, out):
    nc = tc.nc
    with ExitStack() as ctx:
        keep = ctx.enter_context(tc.tile_pool(name="keep", bufs=1))
        stream = ctx.enter_context(tc.tile_pool(name="stream", bufs=3))
        psum1 = ctx.enter_context(tc.psum_pool(name="psum1", bufs=BANK_BUFS))
        psum2 = ctx.enter_context(tc.psum_pool(name="psum2", bufs=4))

        ident = keep.tile([P, P], BF16, name="ident")
        make_identity(nc, ident[:])
        warm_in = keep.tile([P, 1], F32, name="warm_in")
        warm_out = keep.tile([P, 1], F32, name="warm_out")
        nc.gpsimd.memset(warm_in[:], 0.0)
        nc.scalar.activation(out=warm_out[:], in_=warm_in[:], func=RELU)

        ctx.enter_context(tc.manual_schedule())

        x_raw, x_grouped, x_codes, x_scales = {}, {}, {}, {}
        dm_raw, dm_grouped, dm_codes, dm_scales = {}, {}, {}, {}
        banks, d_grouped, d_codes, d_scales = {}, {}, {}, {}
        w_raw, w_grouped, w_codes, w_scales, lifted = {}, {}, {}, {}, {}
        accs, results = {}, {}

        def quantize(codes, scales, grouped):
            nc.vector.quantize_mx(out=codes.bitcast(FP8X4), scales=scales, in_=grouped)

        def load_x(g):
            x_raw[g] = keep.tile([P, PACK, M], BF16, name="x_raw%d" % g)
            nc.sync.dma_start(out=x_raw[g][:], in_=x[g].rearrange("(p j) m -> p j m", j=PACK))

        def load_dm(g, h):
            dm_raw[g, h] = keep.tile([P, PACK, HALF], BF16, name="dm_raw%d%d" % (g, h))
            rows = dispatch_mask[g].rearrange("(p j) e c -> p j (e c)", j=PACK)
            nc.sync.dma_start(out=dm_raw[g, h][:], in_=rows[:, :, h * HALF : (h + 1) * HALF])

        def load_w(e):
            w_raw[e] = stream.tile([P, PACK, H], BF16, name="w_raw", bufs=W_BUFS)
            nc.sync.dma_start(out=w_raw[e][:], in_=wi[e].rearrange("(p j) h -> p j h", j=PACK))

        def group_x(g):
            x_grouped[g] = keep.tile([P, PACK, P, PACK], BF16, name="x_grouped%d" % g, align_bytes=64)
            src = x_raw[g][:].rearrange("p j (m t) -> p t m j", t=PACK)
            nc.vector.tensor_copy(out=x_grouped[g][:, :X_V_SLOTS], in_=src[:, :X_V_SLOTS])
            nc.scalar.copy(out=x_grouped[g][:, X_V_SLOTS:], in_=src[:, X_V_SLOTS:])

        def quant_x(g):
            x_codes[g] = keep.tile([P, M], U32, name="x_codes%d" % g, align_bytes=64)
            x_scales[g] = keep.tile([P, M], U8, name="x_scales%d" % g, align_bytes=64)
            quantize(x_codes[g][:], x_scales[g][:], x_grouped[g][:].rearrange("p t m j -> p (t m j)"))

        def group_dm(g, h):
            dm_grouped[g, h] = keep.tile([P, HALF, PACK], BF16, name="dm_grouped%d%d" % (g, h), align_bytes=64)
            interleave(nc.vector.tensor_copy, dm_grouped[g, h], dm_raw[g, h], 0, DM_V_COLS)
            interleave(nc.scalar.copy, dm_grouped[g, h], dm_raw[g, h], DM_V_COLS, HALF)

        def quant_dm(g, h):
            dm_codes[g, h] = keep.tile([P, HALF], U32, name="dm_codes%d%d" % (g, h), align_bytes=64)
            dm_scales[g, h] = keep.tile([P, HALF], U8, name="dm_scales%d%d" % (g, h), align_bytes=64)
            quantize(dm_codes[g, h][:], dm_scales[g, h][:], dm_grouped[g, h][:].rearrange("p c j -> p (c j)"))
            ready[0] += NB // 2

        def dispatch(g, b):
            banks[g, b] = psum1.tile([P, PACK, P], BANK_DT, name="bank", tag="stage")
            h, q = divmod(b, NB // 2)
            for t in range(PACK):
                nc.tensor.matmul_mx(
                    out=banks[g, b][:, t, :],
                    lhsT=x_codes[g][:, t * P : (t + 1) * P].bitcast(FP8X4),
                    lhsT_scale=x_scales[g][:, t * P : (t + 1) * P],
                    rhs=dm_codes[g, h][:, q * P : (q + 1) * P].bitcast(FP8X4),
                    rhs_scale=dm_scales[g, h][:, q * P : (q + 1) * P],
                    start=True,
                    stop=True,
                )

        def empty_bank(g, b):
            if g == 0:
                d_grouped[b] = keep.tile([P, 2, G, C, PACK], BF16, name="d_grouped%d" % b, align_bytes=64)
            nc.scalar.copy(
                out=d_grouped[b][:, :, g, :, :],
                in_=banks[g, b][:].rearrange("p t (e c) -> p e c t", e=2),
            )

        stage1 = [(g, b) for g in range(G) for b in range(NB)]
        ready, filled, emptied = [0], [0], [0]

        def fill_next():
            if filled[0] < ready[0]:
                dispatch(*stage1[filled[0]])
                filled[0] += 1

        def empty_next(n):
            for i in range(n):
                empty_bank(*stage1[emptied[0]])
                emptied[0] += 1
                fill_next()

        def quant_d(b):
            d_codes[b] = keep.tile([P, 2 * P], U32, name="d_codes%d" % b, align_bytes=64)
            d_scales[b] = keep.tile([P, 2 * P], U8, name="d_scales%d" % b, align_bytes=64)
            quantize(d_codes[b][:], d_scales[b][:], d_grouped[b][:].rearrange("p e g c t -> p (e g c t)"))

        def lift(e):
            lifted[e] = psum1.tile([P, LIFT_COLS, PACK], BF16, name="lifted", tag="stage")
            src = w_raw[e][:, :, H - LIFT_COLS :].rearrange("p t c -> p c t")
            nc.tensor.matmul(out=lifted[e][:], lhsT=ident[:], rhs=src, start=True, stop=True)

        def group_w(e):
            w_grouped[e] = stream.tile([P, H, PACK], BF16, name="w_grouped", align_bytes=64)
            if e < W_V_ONLY:
                interleave(nc.vector.tensor_copy, w_grouped[e], w_raw[e], 0, H)
                return
            interleave(nc.vector.tensor_copy, w_grouped[e], w_raw[e], 0, W_V_COLS)
            interleave(nc.scalar.copy, w_grouped[e], w_raw[e], W_V_COLS, H - LIFT_COLS)
            nc.scalar.copy(out=w_grouped[e][:, H - LIFT_COLS :, :], in_=lifted[e][:])

        def quant_w(e):
            w_codes[e] = stream.tile([P, H], U32, name="w_codes", align_bytes=64)
            w_scales[e] = stream.tile([P, H], U8, name="w_scales", align_bytes=64)
            quantize(w_codes[e][:], w_scales[e][:], w_grouped[e][:].rearrange("p c j -> p (c j)"))

        def project(e):
            b, half = e // 2, e % 2
            for n in range(H // HALF):
                accs[e, n] = psum2.tile([P, HALF], F32, name="acc")
                nc.tensor.matmul_mx(
                    out=accs[e, n][:],
                    lhsT=d_codes[b][:, half * P : (half + 1) * P].bitcast(FP8X4),
                    lhsT_scale=d_scales[b][:, half * P : (half + 1) * P],
                    rhs=w_codes[e][:, n * HALF : (n + 1) * HALF].bitcast(FP8X4),
                    rhs_scale=w_scales[e][:, n * HALF : (n + 1) * HALF],
                    start=True,
                    stop=True,
                )

        def relu_store(e):
            results[e] = stream.tile([P, H], F32, name="result", bufs=6)
            rows = out[e].rearrange("g c h -> (g c) h")
            if e < E - 1:
                for n in range(H // HALF):
                    nc.scalar.activation(out=results[e][:, n * HALF : (n + 1) * HALF], in_=accs[e, n][:], func=RELU)
                nc.sync.dma_start(out=rows, in_=results[e][:])
            else:
                nc.scalar.activation(out=results[e][:, :HALF], in_=accs[e, 0][:], func=RELU)
                nc.vector.tensor_scalar_max(out=results[e][:, HALF:], in0=accs[e, 1][:], scalar1=0.0)
                nc.sync.dma_start(out=rows[:, :HALF], in_=results[e][:, :HALF])
                nc.sync.dma_start(out=rows[:, HALF:], in_=results[e][:, HALF:])

        load_x(0)
        load_x(1)
        for g in range(G):
            for h in range(2):
                load_dm(g, h)
        for e in range(W_BUFS):
            load_w(e)

        group_x(0)
        group_x(1)
        quant_x(0)
        group_dm(0, 0)
        quant_x(1)
        group_dm(0, 1)
        quant_dm(0, 0)
        for i in range(BANK_BUFS):
            fill_next()
        group_dm(1, 0)
        quant_dm(0, 1)
        empty_next(2)
        group_dm(1, 1)
        quant_dm(1, 0)
        empty_next(2)
        group_w(0)
        quant_dm(1, 1)
        empty_next(4)
        group_w(1)
        quant_w(0)
        empty_next(8)
        lift(2)
        for e in range(1, E):
            if e + 2 < E:
                lift(e + 2)
            if e + 1 < E:
                group_w(e + 1)
            if e - 1 + W_BUFS < E:
                load_w(e - 1 + W_BUFS)
            if e == 1:
                quant_d(0)
                project(0)
            if e % 2 == 0:
                quant_d(e // 2)
            quant_w(e)
            project(e)
            relu_store(e - 1)
        relu_store(E - 1)
